import numpy as np
import ml_dtypes


def mxq(x, axis, fmt="e4m3"):
    dtype, down = {"e4m3": (ml_dtypes.float8_e4m3fn, 7), "e5m2": (ml_dtypes.float8_e5m2, 14)}[fmt]
    v = np.moveaxis(np.asarray(x, np.float32).astype(ml_dtypes.bfloat16).astype(np.float64), axis, -1)
    blocks = v.reshape(v.shape[:-1] + (-1, 32))
    amax = np.abs(blocks).max(-1, keepdims=True)
    byte = np.maximum(np.where(amax > 0, np.frexp(amax)[1] - 1 + 127, 0) - down, 1)
    scale = np.exp2(byte - 127.0)
    codes = (blocks / scale).astype(np.float32).astype(dtype).astype(np.float64)
    return np.moveaxis((codes * scale).reshape(v.shape), -1, axis)


WIDE = False


def mx_kscale(k):
    if not WIDE:
        return np.ones(k)
    levels = np.array([10, -10, 5, -5, 0])
    a = np.random.permutation(np.resize(levels, k // 512 * 4)).reshape(k // 512, 4)
    idx = np.arange(k)
    return np.exp2(a[idx // 512, idx % 128 // 32])


BF16 = ml_dtypes.bfloat16


def bf(x):
    return np.asarray(x, np.float32).astype(BF16)


def f64(x):
    return np.asarray(x).astype(np.float64)


B, N, D, H, W = 1, 2048, 1024, 16, 256
HD = D // H
DF = N * HD // W


def setup_inputs():
    s = mx_kscale(D)
    u = mx_kscale(D)
    r = np.concatenate([u, 1.0 / u])
    return {"x": bf(np.random.standard_normal((B, N, D)) * s),
            "Wqk": bf(np.random.standard_normal((2 * D, D)) * 0.8 / np.sqrt(D) * r[:, None] / s)}


def reference(x, Wqk):
    qk = mxq(f64(x), 2, "e4m3") @ mxq(f64(Wqk), 1, "e4m3").T
    qk = qk.reshape(B, N, 2, H, HD).transpose(2, 0, 3, 1, 4)
    q = (qk[0] * HD ** -0.5).reshape(B * H, W, DF)
    k = qk[1].reshape(B * H, W, DF)
    s = mxq(q, 2, "e4m3") @ mxq(k, 2, "e4m3").transpose(0, 2, 1)
    e = np.exp(s - s.max(-1, keepdims=True))
    return e / e.sum(-1, keepdims=True)

@@ -1,0 +1,228 @@
+from contextlib import ExitStack
+
+import concourse.mybir as mybir
+from concourse.masks import make_identity
+
+F32 = mybir.dt.float32
+BF16 = mybir.dt.bfloat16
+I32 = mybir.dt.int32
+U32 = mybir.dt.uint32
+U8 = mybir.dt.uint8
+FP8X4 = mybir.dt.float8_e4m3fn_x4
+ACT = mybir.ActivationFunctionType
+ALU = mybir.AluOpType
+AXIS = mybir.AxisListType
+
+P = 128
+PACK = 4
+K_PASS = P * PACK
+
+TOKENS = 2048
+MODEL = 1024
+HEADS = 16
+HEAD_DIM = 64
+ROWS = 256
+ROW_TOKENS = TOKENS // ROWS
+
+MODEL_PASSES = MODEL // K_PASS
+ROW_PASSES = ROW_TOKENS // PACK
+ROW_BLOCKS = ROWS // P
+GROUPS = ROW_PASSES * ROW_BLOCKS
+GROUP_TOKENS = TOKENS // GROUPS
+PAIRS = HEADS // 2
+QUERY = 0
+KEY = 1
+SCALE = HEAD_DIM ** -0.5
+
+FLOPS = 2 * TOKENS * 2 * MODEL * MODEL + HEADS * 2 * ROWS * ROWS * ROW_TOKENS * HEAD_DIM
+
+
+def tile_slidingwindowattention_pa_kernel(tc, x, Wqk, out):
+    nc = tc.nc
+
+    x_view = x.flatten_outer_dims().rearrange(
+        "(b p a t) k -> a b p t k", b=ROW_BLOCKS, p=P, a=ROW_PASSES, t=PACK
+    )
+    w_view = Wqk.rearrange("(s i p) k -> i p s k", s=2, i=PAIRS, p=P)
+    out_view = out.rearrange("(i h) (b p) v -> i b p h v", h=2, b=ROW_BLOCKS, p=P)
+
+    with ExitStack() as ctx:
+        keep = ctx.enter_context(tc.tile_pool(name="keep", bufs=1))
+        stage = ctx.enter_context(tc.tile_pool(name="stage", bufs=2))
+        small = ctx.enter_context(tc.tile_pool(name="small", bufs=4))
+        results = ctx.enter_context(tc.tile_pool(name="results", bufs=4))
+        flipped = ctx.enter_context(tc.psum_pool(name="flipped", bufs=2))
+        projected = ctx.enter_context(tc.psum_pool(name="projected", bufs=4))
+        scores = ctx.enter_context(tc.psum_pool(name="scores", bufs=2))
+
+        w_raw = [keep.tile([P, 2, MODEL], BF16, name="w_raw%d" % i) for i in range(PAIRS)]
+        x_raw = [keep.tile([P, PACK, MODEL], BF16, name="x_raw%d" % c) for c in range(GROUPS)]
+        nc.sync.dma_start(out=w_raw[0][:], in_=w_view[0])
+        for c in range(GROUPS):
+            nc.sync.dma_start(out=x_raw[c][:], in_=x_view[c // ROW_BLOCKS, c % ROW_BLOCKS])
+        for i in range(1, PAIRS):
+            nc.sync.dma_start(out=w_raw[i][:], in_=w_view[i])
+
+        identity = keep.tile([P, P], F32, name="identity")
+        make_identity(nc, identity[:])
+        warm = keep.tile([P, 1], F32, name="warm")
+        nc.vector.memset(warm[:], 0.0)
+        nc.scalar.activation(out=warm[:], in_=warm[:], func=ACT.Exp)
+
+        q_alone = [
+            [keep.tile([P, ROW_PASSES, ROWS], U32, name="q_alone%d%d" % (n, h), align_bytes=64) for h in range(2)]
+            for n in range(2)
+        ]
+        for n in range(2):
+            for h in range(2):
+                other = slice((1 - h) * HEAD_DIM, (2 - h) * HEAD_DIM)
+                nc.vector.memset(q_alone[n][h][other].bitcast(I32), 0)
+
+        x_codes = [keep.tile([P, MODEL_PASSES, GROUP_TOKENS], U32, name="x_codes%d" % c, align_bytes=64) for c in range(GROUPS)]
+        x_scales = [keep.tile([P, MODEL_PASSES, GROUP_TOKENS], U8, name="x_scales%d" % c, align_bytes=64) for c in range(GROUPS)]
+        w_codes = [keep.tile([P, 2, MODEL_PASSES, P], U32, name="w_codes%d" % i, align_bytes=64) for i in range(PAIRS)]
+        w_scales = [keep.tile([P, 2, MODEL_PASSES, P], U8, name="w_scales%d" % i, align_bytes=64) for i in range(PAIRS)]
+
+        def transpose_words(dst, rows, g, u):
+            first = (2 * g + u) * P
+            nc.tensor.transpose(dst, rows.bitcast(F32)[:, first : first + P], identity[:])
+
+        def prepare_tokens(c):
+            for g in range(MODEL_PASSES):
+                x_grouped = stage.tile([P, GROUP_TOKENS * PACK], BF16, name="x_grouped", align_bytes=64)
+                words = x_grouped[:].bitcast(F32).rearrange("p (r u) -> p r u", u=2)
+                for half in range(2):
+                    bank = flipped.tile([P, 2, 2 * P], F32, name="bank")
+                    for n in range(2):
+                        for u in range(2):
+                            transpose_words(bank[:, u, n * P : (n + 1) * P], x_raw[c][:, 2 * half + n, :], g, u)
+                    columns = slice(half * 2 * P, (half + 1) * 2 * P)
+                    if half == 0:
+                        nc.vector.tensor_copy(out=words[:, columns, :], in_=bank[:].rearrange("p u r -> p r u"))
+                    else:
+                        nc.scalar.copy(out=words[:, columns, :], in_=bank[:].rearrange("p u r -> p r u"))
+                nc.vector.quantize_mx(
+                    out=x_codes[c][:, g, :].bitcast(FP8X4), scales=x_scales[c][:, g, :], in_=x_grouped[:]
+                )
+
+        def prepare_weights(i):
+            w_grouped = stage.tile([P, 2 * MODEL_PASSES * P * PACK], BF16, name="w_grouped", align_bytes=64)
+            words = w_grouped[:].bitcast(F32).rearrange("p (s g m u) -> p s g m u", s=2, g=MODEL_PASSES, u=2)
+            for s in range(2):
+                bank = flipped.tile([P, MODEL_PASSES, 2, P], F32, name="bank")
+                for g in range(MODEL_PASSES):
+                    for u in range(2):
+                        transpose_words(bank[:, g, u, :], w_raw[i][:, s, :], g, u)
+                nc.vector.tensor_copy(out=words[:, s], in_=bank[:].rearrange("p g u m -> p g m u"))
+            nc.vector.quantize_mx(
+                out=w_codes[i][:].rearrange("p s g m -> p (s g m)").bitcast(FP8X4),
+                scales=w_scales[i][:].rearrange("p s g m -> p (s g m)"),
+                in_=w_grouped[:],
+            )
+
+        def project(i, s, c, grouped):
+            a, b = c // ROW_BLOCKS, c % ROW_BLOCKS
+            acc = projected.tile([P, GROUP_TOKENS], F32, name="acc")
+            for g in range(MODEL_PASSES):
+                nc.tensor.matmul_mx(
+                    out=acc[:],
+                    lhsT=w_codes[i][:, s, g, :].bitcast(FP8X4),
+                    lhsT_scale=w_scales[i][:, s, g, :],
+                    rhs=x_codes[c][:, g, :].bitcast(FP8X4),
+                    rhs_scale=x_scales[c][:, g, :],
+                    start=(g == 0),
+                    stop=(g == MODEL_PASSES - 1),
+                )
+            nc.scalar.activation(
+                out=grouped[:, a, b * P : (b + 1) * P, :],
+                in_=acc[:].rearrange("p (t r) -> p r t", t=PACK),
+                func=ACT.Copy,
+                scale=(SCALE if s == QUERY else 1.0),
+            )
+
+        def new_grouped(s):
+            return stage.tile([P, ROW_PASSES, ROWS, PACK], BF16, name="grouped%d" % s, align_bytes=64)
+
+        def quantise_rows(grouped, s):
+            codes = stage.tile([P, ROW_PASSES, ROWS], U32, name="codes%d" % s, align_bytes=64)
+            scales = stage.tile([P, ROW_PASSES, ROWS], U8, name="scales%d" % s, align_bytes=64)
+            nc.vector.quantize_mx(
+                out=codes[:].rearrange("p a w -> p (a w)").bitcast(FP8X4),
+                scales=scales[:].rearrange("p a w -> p (a w)"),
+                in_=grouped[:].rearrange("p a w t -> p (a w t)"),
+            )
+            return codes, scales
+
+        def separate_heads(i, q_codes):
+            for h in range(2):
+                own = slice(h * HEAD_DIM, (h + 1) * HEAD_DIM)
+                nc.vector.tensor_copy(out=q_alone[i % 2][h][own].bitcast(I32), in_=q_codes[own].bitcast(I32))
+
+        def attend(i, q_scales, k_codes, k_scales):
+            for b in range(ROW_BLOCKS):
+                rows = slice(b * P, (b + 1) * P)
+                s_bank = scores.tile([P, 2, ROWS], F32, name="s_bank")
+                for h in range(2):
+                    for a in range(ROW_PASSES):
+                        nc.tensor.matmul_mx(
+                            out=s_bank[:, h, :],
+                            lhsT=q_alone[i % 2][h][:, a, rows].bitcast(FP8X4),
+                            lhsT_scale=q_scales[:, a, rows],
+                            rhs=k_codes[:, a, :].bitcast(FP8X4),
+                            rhs_scale=k_scales[:, a, :],
+                            start=(a == 0),
+                            stop=(a == ROW_PASSES - 1),
+                        )
+                minus_max = small.tile([P, 2], F32, name="minus_max")
+                nc.vector.tensor_reduce(out=minus_max[:], in_=s_bank[:], axis=AXIS.X, op=ALU.max, negate=True)
+                weights = results.tile([P, 2, ROWS], F32, name="weights")
+                sums = small.tile([P, 2], F32, name="sums")
+                for h in range(2):
+                    nc.scalar.activation(
+                        out=weights[:, h, :],
+                        in_=s_bank[:, h, :],
+                        func=ACT.Exp,
+                        bias=minus_max[:, h : h + 1],
+                        scale=1.0,
+                        accum_out=sums[:, h : h + 1],
+                    )
+                inverse = small.tile([P, 2], F32, name="inverse")
+                nc.vector.reciprocal(out=inverse[:], in_=sums[:])
+                for h in range(2):
+                    nc.vector.tensor_scalar(
+                        out=weights[:, h, :],
+                        in0=weights[:, h, :],
+                        scalar1=inverse[:, h : h + 1],
+                        scalar2=None,
+                        op0=ALU.mult,
+                    )
+                nc.sync.dma_start(out=out_view[i, b], in_=weights[:])
+
+        prepare_weights(0)
+        prepare_tokens(0)
+        q_grouped, k_grouped = new_grouped(QUERY), new_grouped(KEY)
+        for c in range(GROUPS):
+            if c + 1 < GROUPS:
+                prepare_tokens(c + 1)
+            else:
+                prepare_weights(1)
+            project(0, QUERY, c, q_grouped)
+            project(0, KEY, c, k_grouped)
+        q_codes, q_scales = quantise_rows(q_grouped, QUERY)
+        separate_heads(0, q_codes)
+
+        for i in range(PAIRS):
+            if i + 2 < PAIRS:
+                prepare_weights(i + 2)
+            k_codes, k_scales = quantise_rows(k_grouped, KEY)
+            if i + 1 < PAIRS:
+                q_grouped = new_grouped(QUERY)
+                for c in range(GROUPS):
+                    project(i + 1, QUERY, c, q_grouped)
+            attend(i, q_scales, k_codes, k_scales)
+            if i + 1 < PAIRS:
+                k_grouped = new_grouped(KEY)
+                for c in range(GROUPS):
+                    project(i + 1, KEY, c, k_grouped)
+                q_codes, q_scales = quantise_rows(q_grouped, QUERY)
+                separate_heads(i + 1, q_codes)

@@ -49,11 +49,11 @@ def tile_slidingwindowattention_pa_kernel(tc, x, Wqk, out):
     with ExitStack() as ctx:
         keep = ctx.enter_context(tc.tile_pool(name="keep", bufs=1))
         stage = ctx.enter_context(tc.tile_pool(name="stage", bufs=2))
-        small = ctx.enter_context(tc.tile_pool(name="small", bufs=4))
-        results = ctx.enter_context(tc.tile_pool(name="results", bufs=4))
-        flipped = ctx.enter_context(tc.psum_pool(name="flipped", bufs=2))
+        small = ctx.enter_context(tc.tile_pool(name="small", bufs=6))
+        results = ctx.enter_context(tc.tile_pool(name="results", bufs=6))
         projected = ctx.enter_context(tc.psum_pool(name="projected", bufs=4))
-        scores = ctx.enter_context(tc.psum_pool(name="scores", bufs=2))
+        shared = ctx.enter_context(tc.psum_pool(name="shared", bufs=4))
+        ctx.enter_context(tc.manual_schedule())
 
         w_raw = [keep.tile([P, 2, MODEL], BF16, name="w_raw%d" % i) for i in range(PAIRS)]
         x_raw = [keep.tile([P, PACK, MODEL], BF16, name="x_raw%d" % c) for c in range(GROUPS)]
@@ -87,12 +87,13 @@ def tile_slidingwindowattention_pa_kernel(tc, x, Wqk, out):
             first = (2 * g + u) * P
             nc.tensor.transpose(dst, rows.bitcast(F32)[:, first : first + P], identity[:])
 
-        def prepare_tokens(c):
+        def flip_tokens(c):
+            grouped = []
             for g in range(MODEL_PASSES):
                 x_grouped = stage.tile([P, GROUP_TOKENS * PACK], BF16, name="x_grouped", align_bytes=64)
                 words = x_grouped[:].bitcast(F32).rearrange("p (r u) -> p r u", u=2)
                 for half in range(2):
-                    bank = flipped.tile([P, 2, 2 * P], F32, name="bank")
+                    bank = shared.tile([P, 2, 2 * P], F32, name="bank")
                     for n in range(2):
                         for u in range(2):
                             transpose_words(bank[:, u, n * P : (n + 1) * P], x_raw[c][:, 2 * half + n, :], g, u)
@@ -101,19 +102,27 @@ def tile_slidingwindowattention_pa_kernel(tc, x, Wqk, out):
                         nc.vector.tensor_copy(out=words[:, columns, :], in_=bank[:].rearrange("p u r -> p r u"))
                     else:
                         nc.scalar.copy(out=words[:, columns, :], in_=bank[:].rearrange("p u r -> p r u"))
+                grouped.append(x_grouped)
+            return grouped
+
+        def quantise_tokens(c, grouped):
+            for g in range(MODEL_PASSES):
                 nc.vector.quantize_mx(
-                    out=x_codes[c][:, g, :].bitcast(FP8X4), scales=x_scales[c][:, g, :], in_=x_grouped[:]
+                    out=x_codes[c][:, g, :].bitcast(FP8X4), scales=x_scales[c][:, g, :], in_=grouped[g][:]
                 )
 
-        def prepare_weights(i):
+        def flip_weights(i):
             w_grouped = stage.tile([P, 2 * MODEL_PASSES * P * PACK], BF16, name="w_grouped", align_bytes=64)
             words = w_grouped[:].bitcast(F32).rearrange("p (s g m u) -> p s g m u", s=2, g=MODEL_PASSES, u=2)
             for s in range(2):
-                bank = flipped.tile([P, MODEL_PASSES, 2, P], F32, name="bank")
+                bank = shared.tile([P, MODEL_PASSES, 2, P], F32, name="bank")
                 for g in range(MODEL_PASSES):
                     for u in range(2):
                         transpose_words(bank[:, g, u, :], w_raw[i][:, s, :], g, u)
                 nc.vector.tensor_copy(out=words[:, s], in_=bank[:].rearrange("p g u m -> p g m u"))
+            return w_grouped
+
+        def quantise_weights(i, w_grouped):
             nc.vector.quantize_mx(
                 out=w_codes[i][:].rearrange("p s g m -> p (s g m)").bitcast(FP8X4),
                 scales=w_scales[i][:].rearrange("p s g m -> p (s g m)"),
@@ -158,10 +167,11 @@ def tile_slidingwindowattention_pa_kernel(tc, x, Wqk, out):
                 own = slice(h * HEAD_DIM, (h + 1) * HEAD_DIM)
                 nc.vector.tensor_copy(out=q_alone[i % 2][h][own].bitcast(I32), in_=q_codes[own].bitcast(I32))
 
-        def attend(i, q_scales, k_codes, k_scales):
+        def score(i, q_scales, k_codes, k_scales):
+            banks = []
             for b in range(ROW_BLOCKS):
                 rows = slice(b * P, (b + 1) * P)
-                s_bank = scores.tile([P, 2, ROWS], F32, name="s_bank")
+                s_bank = shared.tile([P, 2, ROWS], F32, name="bank")
                 for h in range(2):
                     for a in range(ROW_PASSES):
                         nc.tensor.matmul_mx(
@@ -173,8 +183,17 @@ def tile_slidingwindowattention_pa_kernel(tc, x, Wqk, out):
                             start=(a == 0),
                             stop=(a == ROW_PASSES - 1),
                         )
+                banks.append(s_bank)
+            return banks
+
+        def exponentials(banks):
+            maxima = []
+            for s_bank in banks:
                 minus_max = small.tile([P, 2], F32, name="minus_max")
                 nc.vector.tensor_reduce(out=minus_max[:], in_=s_bank[:], axis=AXIS.X, op=ALU.max, negate=True)
+                maxima.append(minus_max)
+            unscaled = []
+            for s_bank, minus_max in zip(banks, maxima):
                 weights = results.tile([P, 2, ROWS], F32, name="weights")
                 sums = small.tile([P, 2], F32, name="sums")
                 for h in range(2):
@@ -186,6 +205,12 @@ def tile_slidingwindowattention_pa_kernel(tc, x, Wqk, out):
                         scale=1.0,
                         accum_out=sums[:, h : h + 1],
                     )
+                unscaled.append((weights, sums))
+            return unscaled
+
+        def normalise_and_store(i, unscaled):
+            for b in range(ROW_BLOCKS):
+                weights, sums = unscaled[b]
                 inverse = small.tile([P, 2], F32, name="inverse")
                 nc.vector.reciprocal(out=inverse[:], in_=sums[:])
                 for h in range(2):
@@ -198,31 +223,41 @@ def tile_slidingwindowattention_pa_kernel(tc, x, Wqk, out):
                     )
                 nc.sync.dma_start(out=out_view[i, b], in_=weights[:])
 
-        prepare_weights(0)
-        prepare_tokens(0)
+        quantise_weights(0, flip_weights(0))
+        quantise_tokens(0, flip_tokens(0))
         q_grouped, k_grouped = new_grouped(QUERY), new_grouped(KEY)
         for c in range(GROUPS):
             if c + 1 < GROUPS:
-                prepare_tokens(c + 1)
+                flipped = flip_tokens(c + 1)
             else:
-                prepare_weights(1)
+                flipped = flip_weights(1)
             project(0, QUERY, c, q_grouped)
             project(0, KEY, c, k_grouped)
+            if c + 1 < GROUPS:
+                quantise_tokens(c + 1, flipped)
+            else:
+                quantise_weights(1, flipped)
         q_codes, q_scales = quantise_rows(q_grouped, QUERY)
         separate_heads(0, q_codes)
 
+        unscaled = None
         for i in range(PAIRS):
             if i + 2 < PAIRS:
-                prepare_weights(i + 2)
+                flipped = flip_weights(i + 2)
             k_codes, k_scales = quantise_rows(k_grouped, KEY)
+            if i + 2 < PAIRS:
+                quantise_weights(i + 2, flipped)
+            if i > 0:
+                normalise_and_store(i - 1, unscaled)
             if i + 1 < PAIRS:
                 q_grouped = new_grouped(QUERY)
                 for c in range(GROUPS):
                     project(i + 1, QUERY, c, q_grouped)
-            attend(i, q_scales, k_codes, k_scales)
+            unscaled = exponentials(score(i, q_scales, k_codes, k_scales))
             if i + 1 < PAIRS:
                 k_grouped = new_grouped(KEY)
                 for c in range(GROUPS):
                     project(i + 1, KEY, c, k_grouped)
                 q_codes, q_scales = quantise_rows(q_grouped, QUERY)
                 separate_heads(i + 1, q_codes)
+        normalise_and_store(PAIRS - 1, unscaled)

@@ -186,12 +186,15 @@ def tile_slidingwindowattention_pa_kernel(tc, x, Wqk, out):
                 banks.append(s_bank)
             return banks
 
-        def exponentials(banks):
+        def row_maxima(banks):
             maxima = []
             for s_bank in banks:
                 minus_max = small.tile([P, 2], F32, name="minus_max")
                 nc.vector.tensor_reduce(out=minus_max[:], in_=s_bank[:], axis=AXIS.X, op=ALU.max, negate=True)
                 maxima.append(minus_max)
+            return maxima
+
+        def exponentials(banks, maxima):
             unscaled = []
             for s_bank, minus_max in zip(banks, maxima):
                 weights = results.tile([P, 2, ROWS], F32, name="weights")
@@ -242,22 +245,25 @@ def tile_slidingwindowattention_pa_kernel(tc, x, Wqk, out):
 
         unscaled = None
         for i in range(PAIRS):
-            if i + 2 < PAIRS:
-                flipped = flip_weights(i + 2)
             k_codes, k_scales = quantise_rows(k_grouped, KEY)
             if i + 2 < PAIRS:
-                quantise_weights(i + 2, flipped)
-            if i > 0:
-                normalise_and_store(i - 1, unscaled)
+                flipped = flip_weights(i + 2)
             if i + 1 < PAIRS:
                 q_grouped = new_grouped(QUERY)
                 for c in range(GROUPS):
                     project(i + 1, QUERY, c, q_grouped)
-            unscaled = exponentials(score(i, q_scales, k_codes, k_scales))
+            banks = score(i, q_scales, k_codes, k_scales)
+            maxima = row_maxima(banks)
+            if i > 0:
+                normalise_and_store(i - 1, unscaled)
             if i + 1 < PAIRS:
                 k_grouped = new_grouped(KEY)
                 for c in range(GROUPS):
                     project(i + 1, KEY, c, k_grouped)
+            unscaled = exponentials(banks, maxima)
+            if i + 2 < PAIRS:
+                quantise_weights(i + 2, flipped)
+            if i + 1 < PAIRS:
                 q_codes, q_scales = quantise_rows(q_grouped, QUERY)
                 separate_heads(i + 1, q_codes)
         normalise_and_store(PAIRS - 1, unscaled)

@@ -32,7 +32,11 @@ GROUP_TOKENS = TOKENS // GROUPS
 PAIRS = HEADS // 2
 QUERY = 0
 KEY = 1
+CODE_WORDS = 2 * ROWS
+SCALE_WORDS = CODE_WORDS // 4
+RECORD = CODE_WORDS + SCALE_WORDS
 SCALE = HEAD_DIM ** -0.5
+ALL_ROWS = slice(0, ROWS)
 
 FLOPS = 2 * TOKENS * 2 * MODEL * MODEL + HEADS * 2 * ROWS * ROWS * ROW_TOKENS * HEAD_DIM
 
@@ -45,6 +49,9 @@ def tile_slidingwindowattention_pa_kernel(tc, x, Wqk, out):
     )
     w_view = Wqk.rearrange("(s i p) k -> i p s k", s=2, i=PAIRS, p=P)
     out_view = out.rearrange("(i h) (b p) v -> i b p h v", h=2, b=ROW_BLOCKS, p=P)
+
+    def partitions(n):
+        return slice(n * HEAD_DIM, (n + 1) * HEAD_DIM)
 
     with ExitStack() as ctx:
         keep = ctx.enter_context(tc.tile_pool(name="keep", bufs=1))
@@ -69,14 +76,15 @@ def tile_slidingwindowattention_pa_kernel(tc, x, Wqk, out):
         nc.vector.memset(warm[:], 0.0)
         nc.scalar.activation(out=warm[:], in_=warm[:], func=ACT.Exp)
 
-        q_alone = [
-            [keep.tile([P, ROW_PASSES, ROWS], U32, name="q_alone%d%d" % (n, h), align_bytes=64) for h in range(2)]
-            for n in range(2)
-        ]
+        packed = [keep.tile([P, ROW_PASSES, RECORD], U32, name="packed%d" % n, align_bytes=64) for n in range(2)]
         for n in range(2):
-            for h in range(2):
-                other = slice((1 - h) * HEAD_DIM, (2 - h) * HEAD_DIM)
-                nc.vector.memset(q_alone[n][h][other].bitcast(I32), 0)
+            nc.vector.memset(packed[n][:, :, CODE_WORDS:].bitcast(I32), 0)
+        joined = [
+            [keep.tile([P, RECORD], U32, name="joined%d%d" % (n, h), align_bytes=64) for h in range(2)] for n in range(2)
+        ]
+        q_alone = [keep.tile([P, ROW_PASSES, ROWS], U32, name="q_alone%d" % h, align_bytes=64) for h in range(2)]
+        for h in range(2):
+            nc.vector.memset(q_alone[h][partitions(1 - h)].bitcast(I32), 0)
 
         x_codes = [keep.tile([P, MODEL_PASSES, GROUP_TOKENS], U32, name="x_codes%d" % c, align_bytes=64) for c in range(GROUPS)]
         x_scales = [keep.tile([P, MODEL_PASSES, GROUP_TOKENS], U8, name="x_scales%d" % c, align_bytes=64) for c in range(GROUPS)]
@@ -98,7 +106,7 @@ def tile_slidingwindowattention_pa_kernel(tc, x, Wqk, out):
                         for u in range(2):
                             transpose_words(bank[:, u, n * P : (n + 1) * P], x_raw[c][:, 2 * half + n, :], g, u)
                     columns = slice(half * 2 * P, (half + 1) * 2 * P)
-                    if half == 0:
+                    if half == 0 and (g == 0 or c % 2 == 0):
                         nc.vector.tensor_copy(out=words[:, columns, :], in_=bank[:].rearrange("p u r -> p r u"))
                     else:
                         nc.scalar.copy(out=words[:, columns, :], in_=bank[:].rearrange("p u r -> p r u"))
@@ -119,7 +127,10 @@ def tile_slidingwindowattention_pa_kernel(tc, x, Wqk, out):
                 for g in range(MODEL_PASSES):
                     for u in range(2):
                         transpose_words(bank[:, g, u, :], w_raw[i][:, s, :], g, u)
-                nc.vector.tensor_copy(out=words[:, s], in_=bank[:].rearrange("p g u m -> p g m u"))
+                if s == QUERY or i > 1:
+                    nc.vector.tensor_copy(out=words[:, s], in_=bank[:].rearrange("p g u m -> p g m u"))
+                else:
+                    nc.scalar.copy(out=words[:, s], in_=bank[:].rearrange("p g u m -> p g m u"))
             return w_grouped
 
         def quantise_weights(i, w_grouped):
@@ -129,8 +140,8 @@ def tile_slidingwindowattention_pa_kernel(tc, x, Wqk, out):
                 in_=w_grouped[:],
             )
 
-        def project(i, s, c, grouped):
-            a, b = c // ROW_BLOCKS, c % ROW_BLOCKS
+        def project(i, s, c, grouped, on_vector=False):
+            b = c % ROW_BLOCKS
             acc = projected.tile([P, GROUP_TOKENS], F32, name="acc")
             for g in range(MODEL_PASSES):
                 nc.tensor.matmul_mx(
@@ -142,128 +153,218 @@ def tile_slidingwindowattention_pa_kernel(tc, x, Wqk, out):
                     start=(g == 0),
                     stop=(g == MODEL_PASSES - 1),
                 )
-            nc.scalar.activation(
-                out=grouped[:, a, b * P : (b + 1) * P, :],
-                in_=acc[:].rearrange("p (t r) -> p r t", t=PACK),
-                func=ACT.Copy,
-                scale=(SCALE if s == QUERY else 1.0),
-            )
+            factor = SCALE if s == QUERY else 1.0
+            by_row = acc[:].rearrange("p (t r) -> p r t", t=PACK)
+            rows = slice(b * P, (b + 1) * P)
+            if on_vector:
+                nc.vector.tensor_scalar(out=grouped[:, s, rows, :], in0=by_row, scalar1=factor, scalar2=None, op0=ALU.mult)
+            else:
+                nc.scalar.activation(out=grouped[:, s, rows, :], in_=by_row, func=ACT.Copy, scale=factor)
 
-        def new_grouped(s):
-            return stage.tile([P, ROW_PASSES, ROWS, PACK], BF16, name="grouped%d" % s, align_bytes=64)
+        def new_grouped():
+            return stage.tile([P, 2, ROWS, PACK], BF16, name="grouped", align_bytes=64)
 
-        def quantise_rows(grouped, s):
-            codes = stage.tile([P, ROW_PASSES, ROWS], U32, name="codes%d" % s, align_bytes=64)
-            scales = stage.tile([P, ROW_PASSES, ROWS], U8, name="scales%d" % s, align_bytes=64)
+        def codes_of(record, s, rows):
+            return record[:, s * ROWS + rows.start : s * ROWS + rows.stop].bitcast(FP8X4)
+
+        def scales_of(record, s, rows):
+            return record[:, CODE_WORDS:].bitcast(U8)[:, s * ROWS + rows.start : s * ROWS + rows.stop]
+
+        def quantise_rows(i, a, grouped):
+            record = packed[i % 2][:, a, :]
             nc.vector.quantize_mx(
-                out=codes[:].rearrange("p a w -> p (a w)").bitcast(FP8X4),
-                scales=scales[:].rearrange("p a w -> p (a w)"),
-                in_=grouped[:].rearrange("p a w t -> p (a w t)"),
+                out=record[:, 0:CODE_WORDS].bitcast(FP8X4),
+                scales=record[:, CODE_WORDS:].bitcast(U8),
+                in_=grouped[:].rearrange("p s w t -> p (s w t)"),
             )
-            return codes, scales
 
-        def separate_heads(i, q_codes):
+        def quantise_part(i, s, a, grouped):
+            record = packed[i % 2][:, a, :]
+            nc.vector.quantize_mx(
+                out=codes_of(record, s, ALL_ROWS),
+                scales=scales_of(record, s, ALL_ROWS),
+                in_=grouped[:, s].rearrange("p w t -> p (w t)"),
+            )
+
+        def join(i, a):
             for h in range(2):
-                own = slice(h * HEAD_DIM, (h + 1) * HEAD_DIM)
-                nc.vector.tensor_copy(out=q_alone[i % 2][h][own].bitcast(I32), in_=q_codes[own].bitcast(I32))
+                nc.sync.dma_start(
+                    out=joined[i % 2][h][partitions(a)].bitcast(I32), in_=packed[i % 2][partitions(h), a].bitcast(I32)
+                )
 
-        def score(i, q_scales, k_codes, k_scales):
-            banks = []
-            for b in range(ROW_BLOCKS):
-                rows = slice(b * P, (b + 1) * P)
-                s_bank = shared.tile([P, 2, ROWS], F32, name="bank")
-                for h in range(2):
-                    for a in range(ROW_PASSES):
-                        nc.tensor.matmul_mx(
-                            out=s_bank[:, h, :],
-                            lhsT=q_alone[i % 2][h][:, a, rows].bitcast(FP8X4),
-                            lhsT_scale=q_scales[:, a, rows],
-                            rhs=k_codes[:, a, :].bitcast(FP8X4),
-                            rhs_scale=k_scales[:, a, :],
-                            start=(a == 0),
-                            stop=(a == ROW_PASSES - 1),
-                        )
-                banks.append(s_bank)
-            return banks
+        def score(i, b):
+            rows = slice(b * P, (b + 1) * P)
+            s_bank = shared.tile([P, 2, ROWS], F32, name="bank")
+            for h in range(2):
+                record = joined[i % 2][h]
+                nc.tensor.matmul_mx(
+                    out=s_bank[:, h, :],
+                    lhsT=codes_of(record, QUERY, rows),
+                    lhsT_scale=scales_of(record, QUERY, rows),
+                    rhs=codes_of(record, KEY, ALL_ROWS),
+                    rhs_scale=scales_of(record, KEY, ALL_ROWS),
+                    start=True,
+                    stop=True,
+                )
+            return s_bank
 
-        def row_maxima(banks):
-            maxima = []
-            for s_bank in banks:
-                minus_max = small.tile([P, 2], F32, name="minus_max")
-                nc.vector.tensor_reduce(out=minus_max[:], in_=s_bank[:], axis=AXIS.X, op=ALU.max, negate=True)
-                maxima.append(minus_max)
-            return maxima
+        def separate_heads(i, a):
+            for h in range(2):
+                own = partitions(h)
+                nc.vector.tensor_copy(out=q_alone[h][own, a, :].bitcast(I32), in_=packed[i % 2][own, a, 0:ROWS].bitcast(I32))
 
-        def exponentials(banks, maxima):
-            unscaled = []
-            for s_bank, minus_max in zip(banks, maxima):
-                weights = results.tile([P, 2, ROWS], F32, name="weights")
-                sums = small.tile([P, 2], F32, name="sums")
-                for h in range(2):
-                    nc.scalar.activation(
-                        out=weights[:, h, :],
-                        in_=s_bank[:, h, :],
-                        func=ACT.Exp,
-                        bias=minus_max[:, h : h + 1],
-                        scale=1.0,
-                        accum_out=sums[:, h : h + 1],
-                    )
-                unscaled.append((weights, sums))
-            return unscaled
+        def score_separated(out, i, b, h, a):
+            rows = slice(b * P, (b + 1) * P)
+            record = packed[i % 2][:, a, :]
+            nc.tensor.matmul_mx(
+                out=out,
+                lhsT=q_alone[h][:, a, rows].bitcast(FP8X4),
+                lhsT_scale=scales_of(record, QUERY, rows),
+                rhs=codes_of(record, KEY, ALL_ROWS),
+                rhs_scale=scales_of(record, KEY, ALL_ROWS),
+                start=(a == 0),
+                stop=(a == ROW_PASSES - 1),
+            )
 
-        def normalise_and_store(i, unscaled):
-            for b in range(ROW_BLOCKS):
-                weights, sums = unscaled[b]
-                inverse = small.tile([P, 2], F32, name="inverse")
-                nc.vector.reciprocal(out=inverse[:], in_=sums[:])
-                for h in range(2):
-                    nc.vector.tensor_scalar(
-                        out=weights[:, h, :],
-                        in0=weights[:, h, :],
-                        scalar1=inverse[:, h : h + 1],
-                        scalar2=None,
-                        op0=ALU.mult,
-                    )
-                nc.sync.dma_start(out=out_view[i, b], in_=weights[:])
+        def row_maxima(s_bank):
+            minus_max = small.tile([P, 2], F32, name="minus_max")
+            nc.vector.tensor_reduce(out=minus_max[:], in_=s_bank[:], axis=AXIS.X, op=ALU.max, negate=True)
+            return minus_max
+
+        def softmax_alone(i, b, h, scores):
+            minus_max = small.tile([P, 1], F32, name="minus_max1")
+            nc.vector.tensor_reduce(out=minus_max[:], in_=scores, axis=AXIS.X, op=ALU.max, negate=True)
+            weights = results.tile([P, ROWS], F32, name="weights1")
+            sums = small.tile([P, 1], F32, name="sums1")
+            nc.scalar.activation(
+                out=weights[:], in_=scores, func=ACT.Exp, bias=minus_max[:], scale=1.0, accum_out=sums[:]
+            )
+            return weights, sums
+
+        def normalise_alone(i, b, h, weights, sums):
+            inverse = small.tile([P, 1], F32, name="inverse1")
+            nc.vector.reciprocal(out=inverse[:], in_=sums[:])
+            nc.vector.tensor_scalar(out=weights[:], in0=weights[:], scalar1=inverse[:], scalar2=None, op0=ALU.mult)
+            nc.sync.dma_start(out=out_view[i, b][:, h], in_=weights[:])
+
+        def exponentials(s_bank, minus_max):
+            weights = results.tile([P, 2, ROWS], F32, name="weights")
+            sums = small.tile([P, 2], F32, name="sums")
+            for h in range(2):
+                nc.scalar.activation(
+                    out=weights[:, h, :],
+                    in_=s_bank[:, h, :],
+                    func=ACT.Exp,
+                    bias=minus_max[:, h : h + 1],
+                    scale=1.0,
+                    accum_out=sums[:, h : h + 1],
+                )
+            return weights, sums
+
+        def normalise_and_store(i, b, weights, sums, engine):
+            inverse = small.tile([P, 2], F32, name="inverse")
+            nc.vector.reciprocal(out=inverse[:], in_=sums[:])
+            for h in range(2):
+                engine.tensor_scalar(
+                    out=weights[:, h, :],
+                    in0=weights[:, h, :],
+                    scalar1=inverse[:, h : h + 1],
+                    scalar2=0.0,
+                    op0=ALU.mult,
+                    op1=ALU.add,
+                )
+            nc.sync.dma_start(out=out_view[i, b], in_=weights[:])
 
         quantise_weights(0, flip_weights(0))
         quantise_tokens(0, flip_tokens(0))
-        q_grouped, k_grouped = new_grouped(QUERY), new_grouped(KEY)
         for c in range(GROUPS):
+            a, b = c // ROW_BLOCKS, c % ROW_BLOCKS
+            if b == 0:
+                grouped = new_grouped()
             if c + 1 < GROUPS:
                 flipped = flip_tokens(c + 1)
             else:
                 flipped = flip_weights(1)
-            project(0, QUERY, c, q_grouped)
-            project(0, KEY, c, k_grouped)
+            project(0, QUERY, c, grouped)
+            project(0, KEY, c, grouped)
             if c + 1 < GROUPS:
                 quantise_tokens(c + 1, flipped)
             else:
                 quantise_weights(1, flipped)
-        q_codes, q_scales = quantise_rows(q_grouped, QUERY)
-        separate_heads(0, q_codes)
+            if b == ROW_BLOCKS - 1:
+                quantise_rows(0, a, grouped)
+                join(0, a)
 
-        unscaled = None
-        for i in range(PAIRS):
-            k_codes, k_scales = quantise_rows(k_grouped, KEY)
-            if i + 2 < PAIRS:
-                flipped = flip_weights(i + 2)
-            if i + 1 < PAIRS:
-                q_grouped = new_grouped(QUERY)
-                for c in range(GROUPS):
-                    project(i + 1, QUERY, c, q_grouped)
-            banks = score(i, q_scales, k_codes, k_scales)
-            maxima = row_maxima(banks)
-            if i > 0:
-                normalise_and_store(i - 1, unscaled)
-            if i + 1 < PAIRS:
-                k_grouped = new_grouped(KEY)
-                for c in range(GROUPS):
-                    project(i + 1, KEY, c, k_grouped)
-            unscaled = exponentials(banks, maxima)
-            if i + 2 < PAIRS:
-                quantise_weights(i + 2, flipped)
-            if i + 1 < PAIRS:
-                q_codes, q_scales = quantise_rows(q_grouped, QUERY)
-                separate_heads(i + 1, q_codes)
-        normalise_and_store(PAIRS - 1, unscaled)
+        banks = None
+        for i in range(1, PAIRS - 1):
+            if banks:
+                maxima = [row_maxima(banks[b]) for b in range(ROW_BLOCKS)]
+                done = [exponentials(banks[0], maxima[0])]
+                quantise_rows(i - 1, 1, grouped)
+                join(i - 1, 1)
+                done.append(exponentials(banks[1], maxima[1]))
+            flipped = flip_weights(i + 1)
+            grouped = new_grouped()
+            project(i, QUERY, 0, grouped)
+            project(i, QUERY, 1, grouped)
+            project(i, KEY, 0, grouped)
+            project(i, KEY, 1, grouped, on_vector=True)
+            if banks:
+                for b in range(ROW_BLOCKS):
+                    normalise_and_store(i - 2, b, done[b][0], done[b][1], nc.vector)
+            quantise_weights(i + 1, flipped)
+            quantise_rows(i, 0, grouped)
+            join(i, 0)
+            grouped = new_grouped()
+            project(i, QUERY, 2, grouped)
+            project(i, QUERY, 3, grouped)
+            project(i, KEY, 2, grouped)
+            project(i, KEY, 3, grouped)
+            banks = [score(i - 1, b) for b in range(ROW_BLOCKS)]
+
+        i = PAIRS - 1
+        maxima = [row_maxima(banks[b]) for b in range(ROW_BLOCKS)]
+        done = [exponentials(banks[0], maxima[0])]
+        quantise_rows(i - 1, 1, grouped)
+        join(i - 1, 1)
+        done.append(exponentials(banks[1], maxima[1]))
+        grouped = new_grouped()
+        project(i, QUERY, 0, grouped)
+        project(i, QUERY, 1, grouped)
+        project(i, KEY, 0, grouped)
+        project(i, KEY, 1, grouped, on_vector=True)
+        for b in range(ROW_BLOCKS):
+            normalise_and_store(i - 2, b, done[b][0], done[b][1], nc.vector)
+        quantise_rows(i, 0, grouped)
+        separate_heads(i, 0)
+        grouped = new_grouped()
+        project(i, QUERY, 2, grouped)
+        project(i, QUERY, 3, grouped)
+        quantise_part(i, QUERY, 1, grouped)
+        separate_heads(i, 1)
+        alone = {}
+        project(i, KEY, 2, grouped)
+        project(i, KEY, 3, grouped)
+        for b in range(ROW_BLOCKS):
+            for h in range(2):
+                pool = projected if b == 0 else shared
+                alone[b, h] = pool.tile([P, GROUP_TOKENS], F32, name=("acc" if b == 0 else "bank"))
+        for b in range(ROW_BLOCKS):
+            for h in range(2):
+                score_separated(alone[b, h][:, 0:ROWS], i, b, h, 0)
+        banks = [score(i - 1, b) for b in range(ROW_BLOCKS)]
+        quantise_part(i, KEY, 1, grouped)
+        for b in range(ROW_BLOCKS):
+            for h in range(2):
+                score_separated(alone[b, h][:, 0:ROWS], i, b, h, 1)
+        maxima = [row_maxima(banks[b]) for b in range(ROW_BLOCKS)]
+        done = [exponentials(banks[b], maxima[b]) for b in range(ROW_BLOCKS)]
+        last_done = {}
+        for b in range(ROW_BLOCKS):
+            for h in range(2):
+                last_done[b, h] = softmax_alone(i, b, h, alone[b, h][:, 0:ROWS])
+        for b in range(ROW_BLOCKS):
+            normalise_and_store(i - 1, b, done[b][0], done[b][1], nc.vector)
+        for b in range(ROW_BLOCKS):
+            for h in range(2):
+                normalise_alone(i, b, h, last_done[b, h][0], last_done[b, h][1])

@@ -64,9 +64,13 @@ def tile_slidingwindowattention_pa_kernel(tc, x, Wqk, out):
 
         w_raw = [keep.tile([P, 2, MODEL], BF16, name="w_raw%d" % i) for i in range(PAIRS)]
         x_raw = [keep.tile([P, PACK, MODEL], BF16, name="x_raw%d" % c) for c in range(GROUPS)]
-        nc.sync.dma_start(out=w_raw[0][:], in_=w_view[0])
+        for s in range(2):
+            nc.sync.dma_start(out=w_raw[0][:, s], in_=w_view[0][:, s])
         for c in range(GROUPS):
-            nc.sync.dma_start(out=x_raw[c][:], in_=x_view[c // ROW_BLOCKS, c % ROW_BLOCKS])
+            pieces = 2 if c < 2 else 1
+            for piece in range(pieces):
+                tokens = slice(piece * PACK // pieces, (piece + 1) * PACK // pieces)
+                nc.sync.dma_start(out=x_raw[c][:, tokens], in_=x_view[c // ROW_BLOCKS, c % ROW_BLOCKS][:, tokens])
         for i in range(1, PAIRS):
             nc.sync.dma_start(out=w_raw[i][:], in_=w_view[i])
 
@@ -82,9 +86,9 @@ def tile_slidingwindowattention_pa_kernel(tc, x, Wqk, out):
         joined = [
             [keep.tile([P, RECORD], U32, name="joined%d%d" % (n, h), align_bytes=64) for h in range(2)] for n in range(2)
         ]
-        q_alone = [keep.tile([P, ROW_PASSES, ROWS], U32, name="q_alone%d" % h, align_bytes=64) for h in range(2)]
+        k_alone = [keep.tile([P, ROW_PASSES, ROWS], U32, name="k_alone%d" % h, align_bytes=64) for h in range(2)]
         for h in range(2):
-            nc.vector.memset(q_alone[h][partitions(1 - h)].bitcast(I32), 0)
+            nc.vector.memset(k_alone[h][partitions(1 - h)].bitcast(I32), 0)
 
         x_codes = [keep.tile([P, MODEL_PASSES, GROUP_TOKENS], U32, name="x_codes%d" % c, align_bytes=64) for c in range(GROUPS)]
         x_scales = [keep.tile([P, MODEL_PASSES, GROUP_TOKENS], U8, name="x_scales%d" % c, align_bytes=64) for c in range(GROUPS)]
@@ -96,21 +100,21 @@ def tile_slidingwindowattention_pa_kernel(tc, x, Wqk, out):
             nc.tensor.transpose(dst, rows.bitcast(F32)[:, first : first + P], identity[:])
 
         def flip_tokens(c):
-            grouped = []
-            for g in range(MODEL_PASSES):
-                x_grouped = stage.tile([P, GROUP_TOKENS * PACK], BF16, name="x_grouped", align_bytes=64)
-                words = x_grouped[:].bitcast(F32).rearrange("p (r u) -> p r u", u=2)
-                for half in range(2):
+            grouped = [
+                stage.tile([P, GROUP_TOKENS * PACK], BF16, name="x_grouped%d" % g, align_bytes=64) for g in range(MODEL_PASSES)
+            ]
+            for half in range(2):
+                for g in range(MODEL_PASSES):
+                    words = grouped[g][:].bitcast(F32).rearrange("p (r u) -> p r u", u=2)
                     bank = shared.tile([P, 2, 2 * P], F32, name="bank")
                     for n in range(2):
                         for u in range(2):
                             transpose_words(bank[:, u, n * P : (n + 1) * P], x_raw[c][:, 2 * half + n, :], g, u)
                     columns = slice(half * 2 * P, (half + 1) * 2 * P)
-                    if half == 0 and (g == 0 or c % 2 == 0):
+                    if g == 0 and (half == 0 or c % 2 == 0):
                         nc.vector.tensor_copy(out=words[:, columns, :], in_=bank[:].rearrange("p u r -> p r u"))
                     else:
                         nc.scalar.copy(out=words[:, columns, :], in_=bank[:].rearrange("p u r -> p r u"))
-                grouped.append(x_grouped)
             return grouped
 
         def quantise_tokens(c, grouped):
@@ -178,12 +182,12 @@ def tile_slidingwindowattention_pa_kernel(tc, x, Wqk, out):
                 in_=grouped[:].rearrange("p s w t -> p (s w t)"),
             )
 
-        def quantise_part(i, s, a, grouped):
+        def quantise_part(i, s, a, grouped, rows):
             record = packed[i % 2][:, a, :]
             nc.vector.quantize_mx(
-                out=codes_of(record, s, ALL_ROWS),
-                scales=scales_of(record, s, ALL_ROWS),
-                in_=grouped[:, s].rearrange("p w t -> p (w t)"),
+                out=codes_of(record, s, rows),
+                scales=scales_of(record, s, rows),
+                in_=grouped[:, s, rows].rearrange("p w t -> p (w t)"),
             )
 
         def join(i, a):
@@ -211,16 +215,16 @@ def tile_slidingwindowattention_pa_kernel(tc, x, Wqk, out):
         def separate_heads(i, a):
             for h in range(2):
                 own = partitions(h)
-                nc.vector.tensor_copy(out=q_alone[h][own, a, :].bitcast(I32), in_=packed[i % 2][own, a, 0:ROWS].bitcast(I32))
+                nc.vector.tensor_copy(out=k_alone[h][own, a, :].bitcast(I32), in_=packed[i % 2][own, a, ROWS : 2 * ROWS].bitcast(I32))
 
         def score_separated(out, i, b, h, a):
             rows = slice(b * P, (b + 1) * P)
             record = packed[i % 2][:, a, :]
             nc.tensor.matmul_mx(
                 out=out,
-                lhsT=q_alone[h][:, a, rows].bitcast(FP8X4),
+                lhsT=codes_of(record, QUERY, rows),
                 lhsT_scale=scales_of(record, QUERY, rows),
-                rhs=codes_of(record, KEY, ALL_ROWS),
+                rhs=k_alone[h][:, a, :].bitcast(FP8X4),
                 rhs_scale=scales_of(record, KEY, ALL_ROWS),
                 start=(a == 0),
                 stop=(a == ROW_PASSES - 1),
@@ -323,48 +327,47 @@ def tile_slidingwindowattention_pa_kernel(tc, x, Wqk, out):
             banks = [score(i - 1, b) for b in range(ROW_BLOCKS)]
 
         i = PAIRS - 1
-        maxima = [row_maxima(banks[b]) for b in range(ROW_BLOCKS)]
-        done = [exponentials(banks[0], maxima[0])]
         quantise_rows(i - 1, 1, grouped)
         join(i - 1, 1)
-        done.append(exponentials(banks[1], maxima[1]))
-        grouped = new_grouped()
-        project(i, QUERY, 0, grouped)
-        project(i, QUERY, 1, grouped)
-        project(i, KEY, 0, grouped)
-        project(i, KEY, 1, grouped, on_vector=True)
+        maxima = [row_maxima(banks[b]) for b in range(ROW_BLOCKS)]
+        grouped = [new_grouped() for a in range(ROW_PASSES)]
+        project(i, KEY, 0, grouped[0])
+        project(i, KEY, 1, grouped[0], on_vector=True)
+        done = [exponentials(banks[b], maxima[b]) for b in range(ROW_BLOCKS)]
+        project(i, KEY, 2, grouped[1])
+        quantise_part(i, KEY, 0, grouped[0], ALL_ROWS)
+        separate_heads(i, 0)
         for b in range(ROW_BLOCKS):
             normalise_and_store(i - 2, b, done[b][0], done[b][1], nc.vector)
-        quantise_rows(i, 0, grouped)
-        separate_heads(i, 0)
-        grouped = new_grouped()
-        project(i, QUERY, 2, grouped)
-        project(i, QUERY, 3, grouped)
-        quantise_part(i, QUERY, 1, grouped)
+        project(i, KEY, 3, grouped[1])
+        project(i, QUERY, 0, grouped[0])
+        quantise_part(i, KEY, 1, grouped[1], ALL_ROWS)
         separate_heads(i, 1)
+        project(i, QUERY, 1, grouped[0])
+        project(i, QUERY, 2, grouped[1])
+        banks = [score(i - 1, b) for b in range(ROW_BLOCKS)]
+        maxima = [row_maxima(banks[0])]
+        quantise_part(i, QUERY, 0, grouped[0], ALL_ROWS)
+        project(i, QUERY, 3, grouped[1])
+        maxima.append(row_maxima(banks[1]))
+        quantise_part(i, QUERY, 1, grouped[1], slice(0, P))
         alone = {}
-        project(i, KEY, 2, grouped)
-        project(i, KEY, 3, grouped)
         for b in range(ROW_BLOCKS):
             for h in range(2):
                 pool = projected if b == 0 else shared
                 alone[b, h] = pool.tile([P, GROUP_TOKENS], F32, name=("acc" if b == 0 else "bank"))
-        for b in range(ROW_BLOCKS):
-            for h in range(2):
                 score_separated(alone[b, h][:, 0:ROWS], i, b, h, 0)
-        banks = [score(i - 1, b) for b in range(ROW_BLOCKS)]
-        quantise_part(i, KEY, 1, grouped)
+        done = [exponentials(banks[0], maxima[0])]
+        quantise_part(i, QUERY, 1, grouped[1], slice(P, ROWS))
+        done.append(exponentials(banks[1], maxima[1]))
         for b in range(ROW_BLOCKS):
             for h in range(2):
                 score_separated(alone[b, h][:, 0:ROWS], i, b, h, 1)
-        maxima = [row_maxima(banks[b]) for b in range(ROW_BLOCKS)]
-        done = [exponentials(banks[b], maxima[b]) for b in range(ROW_BLOCKS)]
         last_done = {}
         for b in range(ROW_BLOCKS):
+            normalise_and_store(i - 1, b, done[b][0], done[b][1], nc.vector)
             for h in range(2):
                 last_done[b, h] = softmax_alone(i, b, h, alone[b, h][:, 0:ROWS])
-        for b in range(ROW_BLOCKS):
-            normalise_and_store(i - 1, b, done[b][0], done[b][1], nc.vector)
         for b in range(ROW_BLOCKS):
             for h in range(2):
                 normalise_alone(i, b, h, last_done[b, h][0], last_done[b, h][1])

@@ -124,13 +124,22 @@ def tile_slidingwindowattention_pa_kernel(tc, x, Wqk, out):
                 )
 
         def flip_weights(i):
-            w_grouped = stage.tile([P, 2 * MODEL_PASSES * P * PACK], BF16, name="w_grouped", align_bytes=64)
-            words = w_grouped[:].bitcast(F32).rearrange("p (s g m u) -> p s g m u", s=2, g=MODEL_PASSES, u=2)
+            return copy_weights(i, transpose_weights(i))
+
+        def transpose_weights(i):
+            banks = []
             for s in range(2):
                 bank = shared.tile([P, MODEL_PASSES, 2, P], F32, name="bank")
                 for g in range(MODEL_PASSES):
                     for u in range(2):
                         transpose_words(bank[:, g, u, :], w_raw[i][:, s, :], g, u)
+                banks.append(bank)
+            return banks
+
+        def copy_weights(i, banks):
+            w_grouped = stage.tile([P, 2 * MODEL_PASSES * P * PACK], BF16, name="w_grouped", align_bytes=64)
+            words = w_grouped[:].bitcast(F32).rearrange("p (s g m u) -> p s g m u", s=2, g=MODEL_PASSES, u=2)
+            for s, bank in enumerate(banks):
                 if s == QUERY or i > 1:
                     nc.vector.tensor_copy(out=words[:, s], in_=bank[:].rearrange("p g u m -> p g m u"))
                 else:
@@ -193,7 +202,8 @@ def tile_slidingwindowattention_pa_kernel(tc, x, Wqk, out):
         def join(i, a):
             for h in range(2):
                 nc.sync.dma_start(
-                    out=joined[i % 2][h][partitions(a)].bitcast(I32), in_=packed[i % 2][partitions(h), a].bitcast(I32)
+                    out=joined[i % 2][h][partitions((a + h) % 2)].bitcast(I32),
+                    in_=packed[i % 2][partitions(h), a].bitcast(I32),
                 )
 
         def score(i, b):
@@ -299,71 +309,77 @@ def tile_slidingwindowattention_pa_kernel(tc, x, Wqk, out):
                 quantise_rows(0, a, grouped)
                 join(0, a)
 
-        banks = None
+        banks, done = None, None
         for i in range(1, PAIRS - 1):
-            if banks:
-                maxima = [row_maxima(banks[b]) for b in range(ROW_BLOCKS)]
-                done = [exponentials(banks[0], maxima[0])]
+            w_banks = transpose_weights(i + 1)
+            if i > 1:
                 quantise_rows(i - 1, 1, grouped)
                 join(i - 1, 1)
-                done.append(exponentials(banks[1], maxima[1]))
-            flipped = flip_weights(i + 1)
+            flipped = copy_weights(i + 1, w_banks)
             grouped = new_grouped()
             project(i, QUERY, 0, grouped)
             project(i, QUERY, 1, grouped)
-            project(i, KEY, 0, grouped)
-            project(i, KEY, 1, grouped, on_vector=True)
-            if banks:
-                for b in range(ROW_BLOCKS):
-                    normalise_and_store(i - 2, b, done[b][0], done[b][1], nc.vector)
             quantise_weights(i + 1, flipped)
+            project(i, KEY, 0, grouped)
+            project(i, KEY, 1, grouped)
+            if i > 1:
+                banks = [score(i - 2, b) for b in range(ROW_BLOCKS)]
+                maxima = [row_maxima(banks[b]) for b in range(ROW_BLOCKS)]
             quantise_rows(i, 0, grouped)
             join(i, 0)
+            if done:
+                for b in range(ROW_BLOCKS):
+                    normalise_and_store(i - 3, b, done[b][0], done[b][1], nc.vector)
             grouped = new_grouped()
             project(i, QUERY, 2, grouped)
             project(i, QUERY, 3, grouped)
             project(i, KEY, 2, grouped)
             project(i, KEY, 3, grouped)
-            banks = [score(i - 1, b) for b in range(ROW_BLOCKS)]
+            if banks:
+                done = [exponentials(banks[b], maxima[b]) for b in range(ROW_BLOCKS)]
 
         i = PAIRS - 1
         quantise_rows(i - 1, 1, grouped)
         join(i - 1, 1)
-        maxima = [row_maxima(banks[b]) for b in range(ROW_BLOCKS)]
+        for b in range(ROW_BLOCKS):
+            normalise_and_store(i - 3, b, done[b][0], done[b][1], nc.vector)
         grouped = [new_grouped() for a in range(ROW_PASSES)]
         project(i, KEY, 0, grouped[0])
         project(i, KEY, 1, grouped[0], on_vector=True)
-        done = [exponentials(banks[b], maxima[b]) for b in range(ROW_BLOCKS)]
         project(i, KEY, 2, grouped[1])
+        project(i, KEY, 3, grouped[1])
+        banks = [score(i - 2, b) for b in range(ROW_BLOCKS)]
         quantise_part(i, KEY, 0, grouped[0], ALL_ROWS)
         separate_heads(i, 0)
-        for b in range(ROW_BLOCKS):
-            normalise_and_store(i - 2, b, done[b][0], done[b][1], nc.vector)
-        project(i, KEY, 3, grouped[1])
+        maxima = [row_maxima(banks[b]) for b in range(ROW_BLOCKS)]
         project(i, QUERY, 0, grouped[0])
+        done = [exponentials(banks[0], maxima[0])]
+        project(i, QUERY, 1, grouped[0])
+        done.append(exponentials(banks[1], maxima[1]))
         quantise_part(i, KEY, 1, grouped[1], ALL_ROWS)
         separate_heads(i, 1)
-        project(i, QUERY, 1, grouped[0])
         project(i, QUERY, 2, grouped[1])
-        banks = [score(i - 1, b) for b in range(ROW_BLOCKS)]
-        maxima = [row_maxima(banks[0])]
         quantise_part(i, QUERY, 0, grouped[0], ALL_ROWS)
+        for b in range(ROW_BLOCKS):
+            normalise_and_store(i - 2, b, done[b][0], done[b][1], nc.vector)
         project(i, QUERY, 3, grouped[1])
-        maxima.append(row_maxima(banks[1]))
-        quantise_part(i, QUERY, 1, grouped[1], slice(0, P))
+        banks = [score(i - 1, b) for b in range(ROW_BLOCKS)]
         alone = {}
         for b in range(ROW_BLOCKS):
             for h in range(2):
                 pool = projected if b == 0 else shared
                 alone[b, h] = pool.tile([P, GROUP_TOKENS], F32, name=("acc" if b == 0 else "bank"))
                 score_separated(alone[b, h][:, 0:ROWS], i, b, h, 0)
+        maxima = [row_maxima(banks[0])]
+        quantise_part(i, QUERY, 1, grouped[1], slice(0, P))
         done = [exponentials(banks[0], maxima[0])]
         quantise_part(i, QUERY, 1, grouped[1], slice(P, ROWS))
+        maxima.append(row_maxima(banks[1]))
         done.append(exponentials(banks[1], maxima[1]))
+        last_done = {}
         for b in range(ROW_BLOCKS):
             for h in range(2):
                 score_separated(alone[b, h][:, 0:ROWS], i, b, h, 1)
-        last_done = {}
         for b in range(ROW_BLOCKS):
             normalise_and_store(i - 1, b, done[b][0], done[b][1], nc.vector)
             for h in range(2):

@@ -329,7 +329,7 @@ def tile_slidingwindowattention_pa_kernel(tc, x, Wqk, out):
             join(i, 0)
             if done:
                 for b in range(ROW_BLOCKS):
-                    normalise_and_store(i - 3, b, done[b][0], done[b][1], nc.vector)
+                    normalise_and_store(i - 3, b, done[b][0], done[b][1], nc.gpsimd)
             grouped = new_grouped()
             project(i, QUERY, 2, grouped)
             project(i, QUERY, 3, grouped)
@@ -342,7 +342,7 @@ def tile_slidingwindowattention_pa_kernel(tc, x, Wqk, out):
         quantise_rows(i - 1, 1, grouped)
         join(i - 1, 1)
         for b in range(ROW_BLOCKS):
-            normalise_and_store(i - 3, b, done[b][0], done[b][1], nc.vector)
+            normalise_and_store(i - 3, b, done[b][0], done[b][1], nc.gpsimd)
         grouped = [new_grouped() for a in range(ROW_PASSES)]
         project(i, KEY, 0, grouped[0])
         project(i, KEY, 1, grouped[0], on_vector=True)
@@ -361,7 +361,7 @@ def tile_slidingwindowattention_pa_kernel(tc, x, Wqk, out):
         project(i, QUERY, 2, grouped[1])
         quantise_part(i, QUERY, 0, grouped[0], ALL_ROWS)
         for b in range(ROW_BLOCKS):
-            normalise_and_store(i - 2, b, done[b][0], done[b][1], nc.vector)
+            normalise_and_store(i - 2, b, done[b][0], done[b][1], nc.gpsimd)
         project(i, QUERY, 3, grouped[1])
         banks = [score(i - 1, b) for b in range(ROW_BLOCKS)]
         alone = {}

@@ -67,9 +67,8 @@ def tile_slidingwindowattention_pa_kernel(tc, x, Wqk, out):
         for s in range(2):
             nc.sync.dma_start(out=w_raw[0][:, s], in_=w_view[0][:, s])
         for c in range(GROUPS):
-            pieces = 2 if c < 2 else 1
-            for piece in range(pieces):
-                tokens = slice(piece * PACK // pieces, (piece + 1) * PACK // pieces)
+            for half in range(2):
+                tokens = slice(half * PACK // 2, (half + 1) * PACK // 2)
                 nc.sync.dma_start(out=x_raw[c][:, tokens], in_=x_view[c // ROW_BLOCKS, c % ROW_BLOCKS][:, tokens])
         for i in range(1, PAIRS):
             nc.sync.dma_start(out=w_raw[i][:], in_=w_view[i])
@@ -319,6 +318,9 @@ def tile_slidingwindowattention_pa_kernel(tc, x, Wqk, out):
             grouped = new_grouped()
             project(i, QUERY, 0, grouped)
             project(i, QUERY, 1, grouped)
+            if done:
+                for b in range(ROW_BLOCKS):
+                    normalise_and_store(i - 3, b, done[b][0], done[b][1], nc.gpsimd)
             quantise_weights(i + 1, flipped)
             project(i, KEY, 0, grouped)
             project(i, KEY, 1, grouped)
@@ -327,9 +329,6 @@ def tile_slidingwindowattention_pa_kernel(tc, x, Wqk, out):
                 maxima = [row_maxima(banks[b]) for b in range(ROW_BLOCKS)]
             quantise_rows(i, 0, grouped)
             join(i, 0)
-            if done:
-                for b in range(ROW_BLOCKS):
-                    normalise_and_store(i - 3, b, done[b][0], done[b][1], nc.gpsimd)
             grouped = new_grouped()
             project(i, QUERY, 2, grouped)
             project(i, QUERY, 3, grouped)

@@ -244,29 +244,22 @@ def tile_slidingwindowattention_pa_kernel(tc, x, Wqk, out):
             nc.vector.tensor_reduce(out=minus_max[:], in_=s_bank[:], axis=AXIS.X, op=ALU.max, negate=True)
             return minus_max
 
-        def softmax_alone(i, b, h, scores):
-            minus_max = small.tile([P, 1], F32, name="minus_max1")
-            nc.vector.tensor_reduce(out=minus_max[:], in_=scores, axis=AXIS.X, op=ALU.max, negate=True)
-            weights = results.tile([P, ROWS], F32, name="weights1")
-            sums = small.tile([P, 1], F32, name="sums1")
-            nc.scalar.activation(
-                out=weights[:], in_=scores, func=ACT.Exp, bias=minus_max[:], scale=1.0, accum_out=sums[:]
-            )
-            return weights, sums
+        def row_maxima_apart(parts):
+            minus_max = small.tile([P, 2], F32, name="minus_max")
+            for h in range(2):
+                nc.vector.tensor_reduce(out=minus_max[:, h : h + 1], in_=parts[h], axis=AXIS.X, op=ALU.max, negate=True)
+            return minus_max
 
-        def normalise_alone(i, b, h, weights, sums):
-            inverse = small.tile([P, 1], F32, name="inverse1")
-            nc.vector.reciprocal(out=inverse[:], in_=sums[:])
-            nc.vector.tensor_scalar(out=weights[:], in0=weights[:], scalar1=inverse[:], scalar2=None, op0=ALU.mult)
-            nc.sync.dma_start(out=out_view[i, b][:, h], in_=weights[:])
+        def heads_of(s_bank):
+            return [s_bank[:, h, :] for h in range(2)]
 
-        def exponentials(s_bank, minus_max):
+        def exponentials(parts, minus_max):
             weights = results.tile([P, 2, ROWS], F32, name="weights")
             sums = small.tile([P, 2], F32, name="sums")
             for h in range(2):
                 nc.scalar.activation(
                     out=weights[:, h, :],
-                    in_=s_bank[:, h, :],
+                    in_=parts[h],
                     func=ACT.Exp,
                     bias=minus_max[:, h : h + 1],
                     scale=1.0,
@@ -274,9 +267,12 @@ def tile_slidingwindowattention_pa_kernel(tc, x, Wqk, out):
                 )
             return weights, sums
 
-        def normalise_and_store(i, b, weights, sums, engine):
+        def invert(sums):
             inverse = small.tile([P, 2], F32, name="inverse")
             nc.vector.reciprocal(out=inverse[:], in_=sums[:])
+            return inverse
+
+        def scale_and_store(i, b, weights, inverse, engine):
             for h in range(2):
                 engine.tensor_scalar(
                     out=weights[:, h, :],
@@ -287,6 +283,11 @@ def tile_slidingwindowattention_pa_kernel(tc, x, Wqk, out):
                     op1=ALU.add,
                 )
             nc.sync.dma_start(out=out_view[i, b], in_=weights[:])
+
+        def normalise_and_store(i, done, engine):
+            inverse = [invert(sums) for weights, sums in done]
+            for b in range(ROW_BLOCKS):
+                scale_and_store(i, b, done[b][0], inverse[b], engine)
 
         quantise_weights(0, flip_weights(0))
         quantise_tokens(0, flip_tokens(0))
@@ -319,8 +320,7 @@ def tile_slidingwindowattention_pa_kernel(tc, x, Wqk, out):
             project(i, QUERY, 0, grouped)
             project(i, QUERY, 1, grouped)
             if done:
-                for b in range(ROW_BLOCKS):
-                    normalise_and_store(i - 3, b, done[b][0], done[b][1], nc.gpsimd)
+                normalise_and_store(i - 3, done, nc.gpsimd)
             quantise_weights(i + 1, flipped)
             project(i, KEY, 0, grouped)
             project(i, KEY, 1, grouped)
@@ -334,55 +334,52 @@ def tile_slidingwindowattention_pa_kernel(tc, x, Wqk, out):
             project(i, QUERY, 3, grouped)
             project(i, KEY, 2, grouped)
             project(i, KEY, 3, grouped)
-            if banks:
-                done = [exponentials(banks[b], maxima[b]) for b in range(ROW_BLOCKS)]
+            if banks and i < PAIRS - 2:
+                done = [exponentials(heads_of(banks[b]), maxima[b]) for b in range(ROW_BLOCKS)]
 
         i = PAIRS - 1
         quantise_rows(i - 1, 1, grouped)
         join(i - 1, 1)
-        for b in range(ROW_BLOCKS):
-            normalise_and_store(i - 3, b, done[b][0], done[b][1], nc.gpsimd)
         grouped = [new_grouped() for a in range(ROW_PASSES)]
         project(i, KEY, 0, grouped[0])
         project(i, KEY, 1, grouped[0], on_vector=True)
-        project(i, KEY, 2, grouped[1])
-        project(i, KEY, 3, grouped[1])
-        banks = [score(i - 2, b) for b in range(ROW_BLOCKS)]
+        done = [exponentials(heads_of(banks[b]), maxima[b]) for b in range(ROW_BLOCKS)]
         quantise_part(i, KEY, 0, grouped[0], ALL_ROWS)
         separate_heads(i, 0)
+        project(i, KEY, 2, grouped[1])
+        project(i, KEY, 3, grouped[1])
+        normalise_and_store(i - 3, done, nc.gpsimd)
+        banks = [score(i - 2, b) for b in range(ROW_BLOCKS)]
         maxima = [row_maxima(banks[b]) for b in range(ROW_BLOCKS)]
         project(i, QUERY, 0, grouped[0])
-        done = [exponentials(banks[0], maxima[0])]
         project(i, QUERY, 1, grouped[0])
-        done.append(exponentials(banks[1], maxima[1]))
+        done = [exponentials(heads_of(banks[b]), maxima[b]) for b in range(ROW_BLOCKS)]
         quantise_part(i, KEY, 1, grouped[1], ALL_ROWS)
         separate_heads(i, 1)
         project(i, QUERY, 2, grouped[1])
         quantise_part(i, QUERY, 0, grouped[0], ALL_ROWS)
-        for b in range(ROW_BLOCKS):
-            normalise_and_store(i - 2, b, done[b][0], done[b][1], nc.gpsimd)
         project(i, QUERY, 3, grouped[1])
+        normalise_and_store(i - 2, done, nc.gpsimd)
         banks = [score(i - 1, b) for b in range(ROW_BLOCKS)]
-        alone = {}
-        for b in range(ROW_BLOCKS):
+        apart = []
+        for b, pool, tag in ((0, projected, "acc"), (1, shared, "bank")):
+            apart.append([pool.tile([P, GROUP_TOKENS], F32, name=tag)[:, 0:ROWS] for h in range(2)])
             for h in range(2):
-                pool = projected if b == 0 else shared
-                alone[b, h] = pool.tile([P, GROUP_TOKENS], F32, name=("acc" if b == 0 else "bank"))
-                score_separated(alone[b, h][:, 0:ROWS], i, b, h, 0)
+                score_separated(apart[b][h], i, b, h, 0)
         maxima = [row_maxima(banks[0])]
         quantise_part(i, QUERY, 1, grouped[1], slice(0, P))
-        done = [exponentials(banks[0], maxima[0])]
         quantise_part(i, QUERY, 1, grouped[1], slice(P, ROWS))
         maxima.append(row_maxima(banks[1]))
-        done.append(exponentials(banks[1], maxima[1]))
-        last_done = {}
-        for b in range(ROW_BLOCKS):
-            for h in range(2):
-                score_separated(alone[b, h][:, 0:ROWS], i, b, h, 1)
-        for b in range(ROW_BLOCKS):
-            normalise_and_store(i - 1, b, done[b][0], done[b][1], nc.vector)
-            for h in range(2):
-                last_done[b, h] = softmax_alone(i, b, h, alone[b, h][:, 0:ROWS])
-        for b in range(ROW_BLOCKS):
-            for h in range(2):
-                normalise_alone(i, b, h, last_done[b, h][0], last_done[b, h][1])
+        for h in range(2):
+            score_separated(apart[0][h], i, 0, h, 1)
+        for h in range(2):
+            score_separated(apart[1][h], i, 1, h, 1)
+        done = [exponentials(heads_of(banks[b]), maxima[b]) for b in range(ROW_BLOCKS)]
+        last_done = [exponentials(apart[b], row_maxima_apart(apart[b])) for b in range(ROW_BLOCKS)]
+        inverse = [invert(sums) for weights, sums in done]
+        scale_and_store(i - 1, 0, done[0][0], inverse[0], nc.vector)
+        last_inverse = [invert(last_done[0][1])]
+        scale_and_store(i - 1, 1, done[1][0], inverse[1], nc.vector)
+        scale_and_store(i, 0, last_done[0][0], last_inverse[0], nc.vector)
+        last_inverse.append(invert(last_done[1][1]))
+        scale_and_store(i, 1, last_done[1][0], last_inverse[1], nc.vector)

@@ -1,3 +1,4 @@
+import math
 from contextlib import ExitStack
 
 import concourse.mybir as mybir
@@ -89,10 +90,21 @@ def tile_slidingwindowattention_pa_kernel(tc, x, Wqk, out):
         for h in range(2):
             nc.vector.memset(k_alone[h][partitions(1 - h)].bitcast(I32), 0)
 
-        x_codes = [keep.tile([P, MODEL_PASSES, GROUP_TOKENS], U32, name="x_codes%d" % c, align_bytes=64) for c in range(GROUPS)]
-        x_scales = [keep.tile([P, MODEL_PASSES, GROUP_TOKENS], U8, name="x_scales%d" % c, align_bytes=64) for c in range(GROUPS)]
-        w_codes = [keep.tile([P, 2, MODEL_PASSES, P], U32, name="w_codes%d" % i, align_bytes=64) for i in range(PAIRS)]
-        w_scales = [keep.tile([P, 2, MODEL_PASSES, P], U8, name="w_scales%d" % i, align_bytes=64) for i in range(PAIRS)]
+        x_codes = [keep.tile([P, MODEL_PASSES, GROUP_TOKENS], U32, name="x_codes%d" % c, align_bytes=256) for c in range(GROUPS)]
+        def shifted(shape, dtype, name, skip):
+            width = math.prod(shape)
+            tile = keep.tile([P, skip + width], dtype, name=name, align_bytes=256)
+            return tile[:, skip:]
+
+        x_scales, w_codes, w_scales = [], [], []
+        for c in range(GROUPS):
+            flat = shifted((MODEL_PASSES, GROUP_TOKENS), U8, "x_scales%d" % c, 64)
+            x_scales.append(flat.rearrange("p (g n) -> p g n", g=MODEL_PASSES))
+        for i in range(PAIRS):
+            flat = shifted((2, MODEL_PASSES, P), U32, "w_codes%d" % i, 48)
+            w_codes.append(flat.rearrange("p (s g m) -> p s g m", s=2, g=MODEL_PASSES))
+            flat = shifted((2, MODEL_PASSES, P), U8, "w_scales%d" % i, 128)
+            w_scales.append(flat.rearrange("p (s g m) -> p s g m", s=2, g=MODEL_PASSES))
 
         def transpose_words(dst, rows, g, u):
             first = (2 * g + u) * P
@@ -147,8 +159,8 @@ def tile_slidingwindowattention_pa_kernel(tc, x, Wqk, out):
 
         def quantise_weights(i, w_grouped):
             nc.vector.quantize_mx(
-                out=w_codes[i][:].rearrange("p s g m -> p (s g m)").bitcast(FP8X4),
-                scales=w_scales[i][:].rearrange("p s g m -> p (s g m)"),
+                out=w_codes[i].rearrange("p s g m -> p (s g m)").bitcast(FP8X4),
+                scales=w_scales[i].rearrange("p s g m -> p (s g m)"),
                 in_=w_grouped[:],
             )
 

import math
from contextlib import ExitStack

import concourse.mybir as mybir
from concourse.masks import make_identity

F32 = mybir.dt.float32
BF16 = mybir.dt.bfloat16
I32 = mybir.dt.int32
U32 = mybir.dt.uint32
U8 = mybir.dt.uint8
FP8X4 = mybir.dt.float8_e4m3fn_x4
ACT = mybir.ActivationFunctionType
ALU = mybir.AluOpType
AXIS = mybir.AxisListType

P = 128
PACK = 4
K_PASS = P * PACK

TOKENS = 2048
MODEL = 1024
HEADS = 16
HEAD_DIM = 64
ROWS = 256
ROW_TOKENS = TOKENS // ROWS

MODEL_PASSES = MODEL // K_PASS
ROW_PASSES = ROW_TOKENS // PACK
ROW_BLOCKS = ROWS // P
GROUPS = ROW_PASSES * ROW_BLOCKS
GROUP_TOKENS = TOKENS // GROUPS
PAIRS = HEADS // 2
QUERY = 0
KEY = 1
CODE_WORDS = 2 * ROWS
SCALE_WORDS = CODE_WORDS // 4
RECORD = CODE_WORDS + SCALE_WORDS
SCALE = HEAD_DIM ** -0.5
ALL_ROWS = slice(0, ROWS)

FLOPS = 2 * TOKENS * 2 * MODEL * MODEL + HEADS * 2 * ROWS * ROWS * ROW_TOKENS * HEAD_DIM


def tile_slidingwindowattention_pa_kernel(tc, x, Wqk, out):
    nc = tc.nc

    x_view = x.flatten_outer_dims().rearrange(
        "(b p a t) k -> a b p t k", b=ROW_BLOCKS, p=P, a=ROW_PASSES, t=PACK
    )
    w_view = Wqk.rearrange("(s i p) k -> i p s k", s=2, i=PAIRS, p=P)
    out_view = out.rearrange("(i h) (b p) v -> i b p h v", h=2, b=ROW_BLOCKS, p=P)

    def partitions(n):
        return slice(n * HEAD_DIM, (n + 1) * HEAD_DIM)

    with ExitStack() as ctx:
        keep = ctx.enter_context(tc.tile_pool(name="keep", bufs=1))
        stage = ctx.enter_context(tc.tile_pool(name="stage", bufs=2))
        small = ctx.enter_context(tc.tile_pool(name="small", bufs=6))
        results = ctx.enter_context(tc.tile_pool(name="results", bufs=6))
        projected = ctx.enter_context(tc.psum_pool(name="projected", bufs=4))
        shared = ctx.enter_context(tc.psum_pool(name="shared", bufs=4))
        ctx.enter_context(tc.manual_schedule())

        w_raw = [keep.tile([P, 2, MODEL], BF16, name="w_raw%d" % i) for i in range(PAIRS)]
        x_raw = [keep.tile([P, PACK, MODEL], BF16, name="x_raw%d" % c) for c in range(GROUPS)]
        for s in range(2):
            nc.sync.dma_start(out=w_raw[0][:, s], in_=w_view[0][:, s])
        for c in range(GROUPS):
            for half in range(2):
                tokens = slice(half * PACK // 2, (half + 1) * PACK // 2)
                nc.sync.dma_start(out=x_raw[c][:, tokens], in_=x_view[c // ROW_BLOCKS, c % ROW_BLOCKS][:, tokens])
        for i in range(1, PAIRS):
            nc.sync.dma_start(out=w_raw[i][:], in_=w_view[i])

        identity = keep.tile([P, P], F32, name="identity")
        make_identity(nc, identity[:])
        warm = keep.tile([P, 1], F32, name="warm")
        nc.vector.memset(warm[:], 0.0)
        nc.scalar.activation(out=warm[:], in_=warm[:], func=ACT.Exp)

        packed = [keep.tile([P, ROW_PASSES, RECORD], U32, name="packed%d" % n, align_bytes=64) for n in range(2)]
        for n in range(2):
            nc.vector.memset(packed[n][:, :, CODE_WORDS:].bitcast(I32), 0)
        joined = [
            [keep.tile([P, RECORD], U32, name="joined%d%d" % (n, h), align_bytes=64) for h in range(2)] for n in range(2)
        ]
        k_alone = [keep.tile([P, ROW_PASSES, ROWS], U32, name="k_alone%d" % h, align_bytes=64) for h in range(2)]
        for h in range(2):
            nc.vector.memset(k_alone[h][partitions(1 - h)].bitcast(I32), 0)

        x_codes = [keep.tile([P, MODEL_PASSES, GROUP_TOKENS], U32, name="x_codes%d" % c, align_bytes=256) for c in range(GROUPS)]
        def shifted(shape, dtype, name, skip):
            width = math.prod(shape)
            tile = keep.tile([P, skip + width], dtype, name=name, align_bytes=256)
            return tile[:, skip:]

        x_scales, w_codes, w_scales = [], [], []
        for c in range(GROUPS):
            flat = shifted((MODEL_PASSES, GROUP_TOKENS), U8, "x_scales%d" % c, 64)
            x_scales.append(flat.rearrange("p (g n) -> p g n", g=MODEL_PASSES))
        for i in range(PAIRS):
            flat = shifted((2, MODEL_PASSES, P), U32, "w_codes%d" % i, 48)
            w_codes.append(flat.rearrange("p (s g m) -> p s g m", s=2, g=MODEL_PASSES))
            flat = shifted((2, MODEL_PASSES, P), U8, "w_scales%d" % i, 128)
            w_scales.append(flat.rearrange("p (s g m) -> p s g m", s=2, g=MODEL_PASSES))

        def transpose_words(dst, rows, g, u):
            first = (2 * g + u) * P
            nc.tensor.transpose(dst, rows.bitcast(F32)[:, first : first + P], identity[:])

        def flip_tokens(c):
            grouped = [
                stage.tile([P, GROUP_TOKENS * PACK], BF16, name="x_grouped%d" % g, align_bytes=64) for g in range(MODEL_PASSES)
            ]
            for half in range(2):
                for g in range(MODEL_PASSES):
                    words = grouped[g][:].bitcast(F32).rearrange("p (r u) -> p r u", u=2)
                    bank = shared.tile([P, 2, 2 * P], F32, name="bank")
                    for n in range(2):
                        for u in range(2):
                            transpose_words(bank[:, u, n * P : (n + 1) * P], x_raw[c][:, 2 * half + n, :], g, u)
                    columns = slice(half * 2 * P, (half + 1) * 2 * P)
                    if g == 0 and (half == 0 or c % 2 == 0):
                        nc.vector.tensor_copy(out=words[:, columns, :], in_=bank[:].rearrange("p u r -> p r u"))
                    else:
                        nc.scalar.copy(out=words[:, columns, :], in_=bank[:].rearrange("p u r -> p r u"))
            return grouped

        def quantise_tokens(c, grouped):
            for g in range(MODEL_PASSES):
                nc.vector.quantize_mx(
                    out=x_codes[c][:, g, :].bitcast(FP8X4), scales=x_scales[c][:, g, :], in_=grouped[g][:]
                )

        def flip_weights(i):
            return copy_weights(i, transpose_weights(i))

        def transpose_weights(i):
            banks = []
            for s in range(2):
                bank = shared.tile([P, MODEL_PASSES, 2, P], F32, name="bank")
                for g in range(MODEL_PASSES):
                    for u in range(2):
                        transpose_words(bank[:, g, u, :], w_raw[i][:, s, :], g, u)
                banks.append(bank)
            return banks

        def copy_weights(i, banks):
            w_grouped = stage.tile([P, 2 * MODEL_PASSES * P * PACK], BF16, name="w_grouped", align_bytes=64)
            words = w_grouped[:].bitcast(F32).rearrange("p (s g m u) -> p s g m u", s=2, g=MODEL_PASSES, u=2)
            for s, bank in enumerate(banks):
                if s == QUERY or i > 1:
                    nc.vector.tensor_copy(out=words[:, s], in_=bank[:].rearrange("p g u m -> p g m u"))
                else:
                    nc.scalar.copy(out=words[:, s], in_=bank[:].rearrange("p g u m -> p g m u"))
            return w_grouped

        def quantise_weights(i, w_grouped):
            nc.vector.quantize_mx(
                out=w_codes[i].rearrange("p s g m -> p (s g m)").bitcast(FP8X4),
                scales=w_scales[i].rearrange("p s g m -> p (s g m)"),
                in_=w_grouped[:],
            )

        def project(i, s, c, grouped, on_vector=False):
            b = c % ROW_BLOCKS
            acc = projected.tile([P, GROUP_TOKENS], F32, name="acc")
            for g in range(MODEL_PASSES):
                nc.tensor.matmul_mx(
                    out=acc[:],
                    lhsT=w_codes[i][:, s, g, :].bitcast(FP8X4),
                    lhsT_scale=w_scales[i][:, s, g, :],
                    rhs=x_codes[c][:, g, :].bitcast(FP8X4),
                    rhs_scale=x_scales[c][:, g, :],
                    start=(g == 0),
                    stop=(g == MODEL_PASSES - 1),
                )
            factor = SCALE if s == QUERY else 1.0
            by_row = acc[:].rearrange("p (t r) -> p r t", t=PACK)
            rows = slice(b * P, (b + 1) * P)
            if on_vector:
                nc.vector.tensor_scalar(out=grouped[:, s, rows, :], in0=by_row, scalar1=factor, scalar2=None, op0=ALU.mult)
            else:
                nc.scalar.activation(out=grouped[:, s, rows, :], in_=by_row, func=ACT.Copy, scale=factor)

        def new_grouped():
            return stage.tile([P, 2, ROWS, PACK], BF16, name="grouped", align_bytes=64)

        def codes_of(record, s, rows):
            return record[:, s * ROWS + rows.start : s * ROWS + rows.stop].bitcast(FP8X4)

        def scales_of(record, s, rows):
            return record[:, CODE_WORDS:].bitcast(U8)[:, s * ROWS + rows.start : s * ROWS + rows.stop]

        def quantise_rows(i, a, grouped):
            record = packed[i % 2][:, a, :]
            nc.vector.quantize_mx(
                out=record[:, 0:CODE_WORDS].bitcast(FP8X4),
                scales=record[:, CODE_WORDS:].bitcast(U8),
                in_=grouped[:].rearrange("p s w t -> p (s w t)"),
            )

        def quantise_part(i, s, a, grouped, rows):
            record = packed[i % 2][:, a, :]
            nc.vector.quantize_mx(
                out=codes_of(record, s, rows),
                scales=scales_of(record, s, rows),
                in_=grouped[:, s, rows].rearrange("p w t -> p (w t)"),
            )

        def join(i, a):
            for h in range(2):
                nc.sync.dma_start(
                    out=joined[i % 2][h][partitions((a + h) % 2)].bitcast(I32),
                    in_=packed[i % 2][partitions(h), a].bitcast(I32),
                )

        def score(i, b):
            rows = slice(b * P, (b + 1) * P)
            s_bank = shared.tile([P, 2, ROWS], F32, name="bank")
            for h in range(2):
                record = joined[i % 2][h]
                nc.tensor.matmul_mx(
                    out=s_bank[:, h, :],
                    lhsT=codes_of(record, QUERY, rows),
                    lhsT_scale=scales_of(record, QUERY, rows),
                    rhs=codes_of(record, KEY, ALL_ROWS),
                    rhs_scale=scales_of(record, KEY, ALL_ROWS),
                    start=True,
                    stop=True,
                )
            return s_bank

        def separate_heads(i, a):
            for h in range(2):
                own = partitions(h)
                nc.vector.tensor_copy(out=k_alone[h][own, a, :].bitcast(I32), in_=packed[i % 2][own, a, ROWS : 2 * ROWS].bitcast(I32))

        def score_separated(out, i, b, h, a):
            rows = slice(b * P, (b + 1) * P)
            record = packed[i % 2][:, a, :]
            nc.tensor.matmul_mx(
                out=out,
                lhsT=codes_of(record, QUERY, rows),
                lhsT_scale=scales_of(record, QUERY, rows),
                rhs=k_alone[h][:, a, :].bitcast(FP8X4),
                rhs_scale=scales_of(record, KEY, ALL_ROWS),
                start=(a == 0),
                stop=(a == ROW_PASSES - 1),
            )

        def row_maxima(s_bank):
            minus_max = small.tile([P, 2], F32, name="minus_max")
            nc.vector.tensor_reduce(out=minus_max[:], in_=s_bank[:], axis=AXIS.X, op=ALU.max, negate=True)
            return minus_max

        def row_maxima_apart(parts):
            minus_max = small.tile([P, 2], F32, name="minus_max")
            for h in range(2):
                nc.vector.tensor_reduce(out=minus_max[:, h : h + 1], in_=parts[h], axis=AXIS.X, op=ALU.max, negate=True)
            return minus_max

        def heads_of(s_bank):
            return [s_bank[:, h, :] for h in range(2)]

        def exponentials(parts, minus_max):
            weights = results.tile([P, 2, ROWS], F32, name="weights")
            sums = small.tile([P, 2], F32, name="sums")
            for h in range(2):
                nc.scalar.activation(
                    out=weights[:, h, :],
                    in_=parts[h],
                    func=ACT.Exp,
                    bias=minus_max[:, h : h + 1],
                    scale=1.0,
                    accum_out=sums[:, h : h + 1],
                )
            return weights, sums

        def invert(sums):
            inverse = small.tile([P, 2], F32, name="inverse")
            nc.vector.reciprocal(out=inverse[:], in_=sums[:])
            return inverse

        def scale_and_store(i, b, weights, inverse, engine):
            for h in range(2):
                engine.tensor_scalar(
                    out=weights[:, h, :],
                    in0=weights[:, h, :],
                    scalar1=inverse[:, h : h + 1],
                    scalar2=0.0,
                    op0=ALU.mult,
                    op1=ALU.add,
                )
            nc.sync.dma_start(out=out_view[i, b], in_=weights[:])

        def normalise_and_store(i, done, engine):
            inverse = [invert(sums) for weights, sums in done]
            for b in range(ROW_BLOCKS):
                scale_and_store(i, b, done[b][0], inverse[b], engine)

        quantise_weights(0, flip_weights(0))
        quantise_tokens(0, flip_tokens(0))
        for c in range(GROUPS):
            a, b = c // ROW_BLOCKS, c % ROW_BLOCKS
            if b == 0:
                grouped = new_grouped()
            if c + 1 < GROUPS:
                flipped = flip_tokens(c + 1)
            else:
                flipped = flip_weights(1)
            project(0, QUERY, c, grouped)
            project(0, KEY, c, grouped)
            if c + 1 < GROUPS:
                quantise_tokens(c + 1, flipped)
            else:
                quantise_weights(1, flipped)
            if b == ROW_BLOCKS - 1:
                quantise_rows(0, a, grouped)
                join(0, a)

        banks, done = None, None
        for i in range(1, PAIRS - 1):
            w_banks = transpose_weights(i + 1)
            if i > 1:
                quantise_rows(i - 1, 1, grouped)
                join(i - 1, 1)
            flipped = copy_weights(i + 1, w_banks)
            grouped = new_grouped()
            project(i, QUERY, 0, grouped)
            project(i, QUERY, 1, grouped)
            if done:
                normalise_and_store(i - 3, done, nc.gpsimd)
            quantise_weights(i + 1, flipped)
            project(i, KEY, 0, grouped)
            project(i, KEY, 1, grouped)
            if i > 1:
                banks = [score(i - 2, b) for b in range(ROW_BLOCKS)]
                maxima = [row_maxima(banks[b]) for b in range(ROW_BLOCKS)]
            quantise_rows(i, 0, grouped)
            join(i, 0)
            grouped = new_grouped()
            project(i, QUERY, 2, grouped)
            project(i, QUERY, 3, grouped)
            project(i, KEY, 2, grouped)
            project(i, KEY, 3, grouped)
            if banks and i < PAIRS - 2:
                done = [exponentials(heads_of(banks[b]), maxima[b]) for b in range(ROW_BLOCKS)]

        i = PAIRS - 1
        quantise_rows(i - 1, 1, grouped)
        join(i - 1, 1)
        grouped = [new_grouped() for a in range(ROW_PASSES)]
        project(i, KEY, 0, grouped[0])
        project(i, KEY, 1, grouped[0], on_vector=True)
        done = [exponentials(heads_of(banks[b]), maxima[b]) for b in range(ROW_BLOCKS)]
        quantise_part(i, KEY, 0, grouped[0], ALL_ROWS)
        separate_heads(i, 0)
        project(i, KEY, 2, grouped[1])
        project(i, KEY, 3, grouped[1])
        normalise_and_store(i - 3, done, nc.gpsimd)
        banks = [score(i - 2, b) for b in range(ROW_BLOCKS)]
        maxima = [row_maxima(banks[b]) for b in range(ROW_BLOCKS)]
        project(i, QUERY, 0, grouped[0])
        project(i, QUERY, 1, grouped[0])
        done = [exponentials(heads_of(banks[b]), maxima[b]) for b in range(ROW_BLOCKS)]
        quantise_part(i, KEY, 1, grouped[1], ALL_ROWS)
        separate_heads(i, 1)
        project(i, QUERY, 2, grouped[1])
        quantise_part(i, QUERY, 0, grouped[0], ALL_ROWS)
        project(i, QUERY, 3, grouped[1])
        normalise_and_store(i - 2, done, nc.gpsimd)
        banks = [score(i - 1, b) for b in range(ROW_BLOCKS)]
        apart = []
        for b, pool, tag in ((0, projected, "acc"), (1, shared, "bank")):
            apart.append([pool.tile([P, GROUP_TOKENS], F32, name=tag)[:, 0:ROWS] for h in range(2)])
            for h in range(2):
                score_separated(apart[b][h], i, b, h, 0)
        maxima = [row_maxima(banks[0])]
        quantise_part(i, QUERY, 1, grouped[1], slice(0, P))
        quantise_part(i, QUERY, 1, grouped[1], slice(P, ROWS))
        maxima.append(row_maxima(banks[1]))
        for h in range(2):
            score_separated(apart[0][h], i, 0, h, 1)
        for h in range(2):
            score_separated(apart[1][h], i, 1, h, 1)
        done = [exponentials(heads_of(banks[b]), maxima[b]) for b in range(ROW_BLOCKS)]
        last_done = [exponentials(apart[b], row_maxima_apart(apart[b])) for b in range(ROW_BLOCKS)]
        inverse = [invert(sums) for weights, sums in done]
        scale_and_store(i - 1, 0, done[0][0], inverse[0], nc.vector)
        last_inverse = [invert(last_done[0][1])]
        scale_and_store(i - 1, 1, done[1][0], inverse[1], nc.vector)
        scale_and_store(i, 0, last_done[0][0], last_inverse[0], nc.vector)
        last_inverse.append(invert(last_done[1][1]))
        scale_and_store(i, 1, last_done[1][0], last_inverse[1], nc.vector)
